import numpy as np
import ml_dtypes


def mxq(x, axis, fmt="e4m3"):
    dtype, down = {"e4m3": (ml_dtypes.float8_e4m3fn, 7), "e5m2": (ml_dtypes.float8_e5m2, 14)}[fmt]
    v = np.moveaxis(np.asarray(x, np.float32).astype(ml_dtypes.bfloat16).astype(np.float64), axis, -1)
    blocks = v.reshape(v.shape[:-1] + (-1, 32))
    amax = np.abs(blocks).max(-1, keepdims=True)
    byte = np.maximum(np.where(amax > 0, np.frexp(amax)[1] - 1 + 127, 0) - down, 1)
    scale = np.exp2(byte - 127.0)
    codes = (blocks / scale).astype(np.float32).astype(dtype).astype(np.float64)
    return np.moveaxis((codes * scale).reshape(v.shape), -1, axis)


WIDE = False


def mx_kscale(k):
    if not WIDE:
        return np.ones(k)
    levels = np.array([10, -10, 5, -5, 0])
    a = np.random.permutation(np.resize(levels, k // 512 * 4)).reshape(k // 512, 4)
    idx = np.arange(k)
    return np.exp2(a[idx // 512, idx % 128 // 32])


BF16 = ml_dtypes.bfloat16


def bf(x):
    return np.asarray(x, np.float32).astype(BF16)


def f64(x):
    return np.asarray(x).astype(np.float64)


N, S, I, L, M = 64, 4, 7680, 512, 256
D = I + L


def sigmoid(v):
    return 1.0 / (1.0 + np.exp(-v))


def setup_inputs():
    s = mx_kscale(D)
    r = np.random.standard_normal
    return {"modulation": bf((r((N, S, I)) * s[:I]).reshape(N, S * I)),
            "h0": bf((r((N, S, L)) * s[I:]).reshape(N, S * L)),
            "c_new": bf(0.75 * r((N, S * L))),
            "Wo": bf(r((S, L, D)) / np.sqrt(D) / s), "b_o": bf(0.3 * r((S, L))),
            "Wy": bf(r((S, M, L)) * 2.0 / np.sqrt(L)), "b_y": bf(0.2 * r((S, M)))}


def proj(aq, W, b):
    return (aq.transpose(1, 0, 2) @ mxq(f64(W), 2, "e4m3").transpose(0, 2, 1)).transpose(1, 0, 2) + f64(b)


def reference(modulation, h0, c_new, Wo, b_o, Wy, b_y):
    x = f64(modulation).reshape(N, S, I)
    h = f64(h0).reshape(N, S, L)
    c = f64(c_new).reshape(N, S, L)
    xq = mxq(np.concatenate([x, h], axis=-1), 2, "e4m3")
    o = sigmoid(proj(xq, Wo, b_o))
    h_new = o * np.tanh(c)
    y = proj(mxq(h_new, 2, "e4m3"), Wy, b_y)
    return y.reshape(N, S * M)

@@ -1,0 +1,277 @@
+from contextlib import ExitStack
+
+import concourse.mybir as mybir
+from concourse.masks import make_identity
+
+F32 = mybir.dt.float32
+BF16 = mybir.dt.bfloat16
+U32 = mybir.dt.uint32
+U8 = mybir.dt.uint8
+I32 = mybir.dt.int32
+FP8X4 = mybir.dt.float8_e4m3fn_x4
+ACT = mybir.ActivationFunctionType
+ALU = mybir.AluOpType
+
+P = 128
+PACK = 4
+K_PASS = P * PACK
+BANK = 512
+
+ROWS = 64
+STREAMS = 4
+X_FEAT = 7680
+HID = 512
+OUT_FEAT = 256
+DEPTH = X_FEAT + HID
+
+FLOPS = 2 * ROWS * STREAMS * (DEPTH * HID + HID * OUT_FEAT)
+
+CHUNK = DEPTH // 2
+CHUNK_PASSES = CHUNK // K_PASS
+CHUNK_BANKS = CHUNK // 2 // BANK
+CHUNK_WORDS = CHUNK // PACK
+GATE_BLOCKS = HID // P
+PAIR_UNITS = 1 + 2 * GATE_BLOCKS
+N_CHUNKS = 2 * PAIR_UNITS * 2
+
+RAW_BUFS = 12
+VECTOR_BANK = 2
+
+
+def tile_flatlstm_pb_k_kernel(tc, modulation, h0, c_new, Wo, b_o, Wy, b_y, out):
+    nc = tc.nc
+
+    x_view = modulation.rearrange("n (a b i) -> (n a) b i", a=2, b=2)
+    h_view = h0.rearrange("n (a b l) -> (n a) b l", a=2, b=2)
+    c_view = c_new.rearrange("n (a c) -> (n a) c", a=2)
+    wo_view = Wo.rearrange("s (j t) k -> s t j k", t=GATE_BLOCKS)
+    wy_view = Wy.rearrange("s (h m) k -> m (s h) k", m=P)
+
+    with ExitStack() as ctx:
+        keep = ctx.enter_context(tc.tile_pool(name="keep", bufs=1))
+        raw_pool = ctx.enter_context(tc.tile_pool(name="raw", bufs=RAW_BUFS))
+        grouped_pool = ctx.enter_context(tc.tile_pool(name="grouped", bufs=3))
+        xh_pool = ctx.enter_context(tc.tile_pool(name="xh", bufs=2))
+        wo_pool = ctx.enter_context(tc.tile_pool(name="wo", bufs=3))
+        gate_pool = ctx.enter_context(tc.tile_pool(name="gate", bufs=2))
+        flip_psum = ctx.enter_context(tc.psum_pool(name="flip", bufs=6))
+        sum_psum = ctx.enter_context(tc.psum_pool(name="sums", bufs=2))
+        ctx.enter_context(tc.manual_schedule())
+
+        def flip_bank(blocks, dest_words, bank):
+            flipped = flip_psum.tile([P, BANK], F32)
+            for j, block in enumerate(blocks):
+                nc.tensor.transpose(flipped[:, j * P : (j + 1) * P], block, ident[:])
+            src = flipped[:].rearrange("p (g u c) -> p g c u", g=2, u=2)
+            dst = dest_words.rearrange("p (g c u) -> p g c u", g=2, u=2)
+            if bank % CHUNK_BANKS == VECTOR_BANK:
+                nc.vector.tensor_copy(out=dst, in_=src)
+            else:
+                nc.scalar.copy(out=dst, in_=src)
+
+        def place(i):
+            unit, half = divmod(i, 2)
+            b, r = divmod(unit, PAIR_UNITS)
+            return b, r, half
+
+        def stream_block(b, r):
+            a, t = divmod(r - 1, GATE_BLOCKS)
+            return a, 2 * a + b, t
+
+        raws, groupeds, xh_codes, wo_codes, sums, gates = {}, {}, {}, {}, {}, {}
+
+        def load(i):
+            b, r, half = place(i)
+            raw = raw_pool.tile([P, CHUNK], BF16)
+            if r > 0:
+                a, s, t = stream_block(b, r)
+                nc.sync.dma_start(out=raw[:], in_=wo_view[s, t, :, half * CHUNK : (half + 1) * CHUNK])
+            elif half == 0:
+                nc.sync.dma_start(out=raw[:], in_=x_view[:, b, 0:CHUNK])
+            else:
+                nc.sync.dma_start(out=raw[:, 0 : X_FEAT - CHUNK], in_=x_view[:, b, CHUNK:X_FEAT])
+                nc.sync.dma_start(out=raw[:, X_FEAT - CHUNK : CHUNK], in_=h_view[:, b, :])
+            raws[i] = raw
+
+        def flip(i):
+            raw_words = raws[i][:].bitcast(F32)
+            grouped = grouped_pool.tile([P, CHUNK], BF16, align_bytes=64)
+            grouped_words = grouped[:].bitcast(F32)
+            for bank in range(CHUNK_BANKS):
+                first = bank * BANK
+                blocks = [raw_words[:, first + j * P : first + (j + 1) * P] for j in range(4)]
+                flip_bank(blocks, grouped_words[:, first : first + BANK], bank)
+            groupeds[i] = grouped
+
+        def quantise(i):
+            b, r, half = place(i)
+            if r == 0:
+                if half == 0:
+                    xq = xh_pool.tile([P, 2 * CHUNK_WORDS], U32, align_bytes=64)
+                    xs = xh_pool.tile([P, 2 * CHUNK_WORDS], U8, align_bytes=64)
+                    xh_codes[b] = (xq, xs)
+                xq, xs = xh_codes[b]
+                cols = slice(half * CHUNK_WORDS, (half + 1) * CHUNK_WORDS)
+                codes, scales = xq[:, cols], xs[:, cols]
+            else:
+                wq = wo_pool.tile([P, CHUNK_WORDS], U32, align_bytes=64)
+                ws = wo_pool.tile([P, CHUNK_WORDS], U8, align_bytes=64)
+                wo_codes[i] = (wq, ws)
+                codes, scales = wq[:], ws[:]
+            nc.vector.quantize_mx(out=codes.bitcast(FP8X4), scales=scales, in_=groupeds[i][:])
+
+        def multiply(i):
+            b, r, half = place(i)
+            if r == 0:
+                return
+            a, s, t = stream_block(b, r)
+            wq, ws = wo_codes[i]
+            xq, xs = xh_codes[b]
+            if half == 0:
+                acc = sum_psum.tile([P, P], F32, tag="sum")
+                sums[s] = acc
+            acc = sums[s]
+            for g in range(CHUNK_PASSES):
+                w_cols = slice(g * P, (g + 1) * P)
+                x_cols = slice((half * CHUNK_PASSES + g) * P, (half * CHUNK_PASSES + g + 1) * P)
+                nc.tensor.matmul_mx(
+                    out=acc[:],
+                    lhsT=wq[:, w_cols].bitcast(FP8X4),
+                    lhsT_scale=ws[:, w_cols],
+                    rhs=xq[:, x_cols].bitcast(FP8X4),
+                    rhs_scale=xs[:, x_cols],
+                    start=(half == 0 and g == 0),
+                    stop=(half == 1 and g == CHUNK_PASSES - 1),
+                )
+            if half == 0:
+                return
+            if t == 0:
+                gate = gate_pool.tile([P, GATE_BLOCKS, ROWS], F32)
+                gates[s] = gate
+            gate = gates[s]
+            nc.scalar.activation(
+                out=gate[:, t, :],
+                in_=acc[:].rearrange("p (n a) -> p a n", a=2)[:, a, :],
+                func=ACT.Sigmoid,
+                bias=bias_o[:, s * GATE_BLOCKS + t : s * GATE_BLOCKS + t + 1],
+            )
+            if t < GATE_BLOCKS - 1:
+                return
+            h_new = gate_pool.tile([P, ROWS * PACK], BF16, align_bytes=64)
+            nc.vector.tensor_tensor(
+                out=h_new[:].rearrange("p (n t) -> p n t", t=PACK),
+                in0=gate[:].rearrange("p t n -> p n t"),
+                in1=tanh_c[:, s, :].rearrange("p (n t) -> p n t", t=PACK),
+                op=ALU.mult,
+            )
+            nc.vector.quantize_mx(
+                out=hq[:, s, 0:ROWS].bitcast(FP8X4), scales=hs[:, s, 0:ROWS], in_=h_new[:]
+            )
+
+        def project(i):
+            b, r, half = place(i)
+            if r == 0 or half == 0:
+                return
+            a, s, t = stream_block(b, r)
+            if t < GATE_BLOCKS - 1:
+                return
+            y_sum = sum_psum.tile([P, OUT_FEAT], F32, tag="sum")
+            nc.tensor.matmul_mx(
+                out=y_sum[:],
+                lhsT=hq[:, s, :].bitcast(FP8X4),
+                lhsT_scale=hs[:, s, :],
+                rhs=wyq[:, s, :].bitcast(FP8X4),
+                rhs_scale=wys[:, s, :],
+                start=True,
+                stop=True,
+            )
+            y = gate_pool.tile([ROWS, OUT_FEAT], F32)
+            nc.vector.tensor_tensor(
+                out=y[:], in0=y_sum[0:ROWS, :], in1=bias_y[0:ROWS, s, :], op=ALU.add
+            )
+            nc.sync.dma_start(out=out[:, s * OUT_FEAT : (s + 1) * OUT_FEAT], in_=y[:])
+
+        ident = keep.tile([P, P], F32)
+        make_identity(nc, ident[:])
+        ones = keep.tile([P, P], BF16)
+        nc.vector.memset(ones[:], 1.0)
+        hq = keep.tile([P, STREAMS, P], U32, align_bytes=64)
+        hs = keep.tile([P, STREAMS, P], U8, align_bytes=64)
+        nc.vector.memset(hq[:].bitcast(I32), 0)
+        nc.vector.memset(hs[:].bitcast(I32), 0)
+        by_row = keep.tile([P, STREAMS * OUT_FEAT], BF16)
+        nc.vector.memset(by_row[:], 0.0)
+
+        nc.scalar.dma_start(out=by_row[0:1, :], in_=b_y.rearrange("(o s) m -> o (s m)", o=1))
+        bo_bf16 = keep.tile([P, STREAMS * GATE_BLOCKS], BF16)
+        nc.scalar.dma_start(
+            out=bo_bf16[:].rearrange("p (s t) -> p s t", t=GATE_BLOCKS),
+            in_=b_o.rearrange("s (p t) -> p s t", t=GATE_BLOCKS),
+        )
+        c_raw = keep.tile([P, 2 * HID], BF16)
+        nc.sync.dma_start(out=c_raw[:], in_=c_view)
+        wy_raw = keep.tile([P, 2 * STREAMS, HID], BF16)
+        nc.sync.dma_start(out=wy_raw[:], in_=wy_view)
+        for i in range(RAW_BUFS):
+            load(i)
+
+        bias_o = keep.tile([P, STREAMS * GATE_BLOCKS], F32)
+        nc.vector.tensor_copy(out=bias_o[:], in_=bo_bf16[:])
+
+        bias_y = keep.tile([P, STREAMS, OUT_FEAT], F32)
+        for half in range(STREAMS * OUT_FEAT // BANK):
+            spread = flip_psum.tile([P, BANK], F32, tag="flipped")
+            nc.tensor.matmul(
+                out=spread[:], lhsT=ones[:], rhs=by_row[:, half * BANK : (half + 1) * BANK],
+                start=True, stop=True,
+            )
+            nc.vector.tensor_copy(
+                out=bias_y[:].rearrange("p s m -> p (s m)")[:, half * BANK : (half + 1) * BANK],
+                in_=spread[:],
+            )
+
+        c_words = c_raw[:].bitcast(F32).rearrange("r (b p u) -> r b u p", b=2, u=2)
+        c_flipped = flip_psum.tile([P, BANK], F32, tag="flipped")
+        for b in range(2):
+            for u in range(2):
+                j = 2 * b + u
+                nc.tensor.transpose(c_flipped[:, j * P : (j + 1) * P], c_words[:, b, u, :], ident[:])
+        c_values = c_flipped[:].bitcast(BF16).rearrange(
+            "p (b u n a e) -> p b a n u e", b=2, u=2, a=2, e=2
+        )
+        tanh_c = keep.tile([P, STREAMS, ROWS * PACK], F32)
+        for s in range(STREAMS):
+            a, b = divmod(s, 2)
+            nc.scalar.activation(
+                out=tanh_c[:, s, :].rearrange("p (n u e) -> p n u e", u=2, e=2),
+                in_=c_values[:, b, a],
+                func=ACT.Tanh,
+            )
+
+        wy_words = wy_raw[:].rearrange("m r k -> m (r k)").bitcast(F32).rearrange(
+            "m (r p u) -> m r u p", r=2 * STREAMS, u=2
+        )
+        wy_grouped = grouped_pool.tile([P, STREAMS * OUT_FEAT * PACK], BF16, align_bytes=64, tag="grouped")
+        wy_grouped_words = wy_grouped[:].bitcast(F32)
+        for s in range(STREAMS):
+            blocks = [wy_words[:, 2 * s + h, u, :] for h in range(2) for u in range(2)]
+            flip_bank(blocks, wy_grouped_words[:, s * BANK : (s + 1) * BANK], s)
+        wyq = keep.tile([P, STREAMS, OUT_FEAT], U32, align_bytes=64)
+        wys = keep.tile([P, STREAMS, OUT_FEAT], U8, align_bytes=64)
+        nc.vector.quantize_mx(
+            out=wyq[:].rearrange("p s m -> p (s m)").bitcast(FP8X4),
+            scales=wys[:].rearrange("p s m -> p (s m)"),
+            in_=wy_grouped[:],
+        )
+
+        for i in range(N_CHUNKS + 3):
+            if 0 <= i - 1 < N_CHUNKS:
+                quantise(i - 1)
+            if i < N_CHUNKS:
+                flip(i)
+            if i + RAW_BUFS < N_CHUNKS:
+                load(i + RAW_BUFS)
+            if 0 <= i - 2 < N_CHUNKS:
+                multiply(i - 2)
+            if 0 <= i - 3 < N_CHUNKS:
+                project(i - 3)

@@ -195,6 +195,8 @@ def tile_flatlstm_pb_k_kernel(tc, modulation, h0, c_new, Wo, b_o, Wy, b_y, out):
         make_identity(nc, ident[:])
         ones = keep.tile([P, P], BF16)
         nc.vector.memset(ones[:], 1.0)
+        bo_rows = keep.tile([P, HID], BF16)
+        nc.vector.memset(bo_rows[:], 0.0)
         hq = keep.tile([P, STREAMS, P], U32, align_bytes=64)
         hs = keep.tile([P, STREAMS, P], U8, align_bytes=64)
         nc.vector.memset(hq[:].bitcast(I32), 0)
@@ -202,33 +204,30 @@ def tile_flatlstm_pb_k_kernel(tc, modulation, h0, c_new, Wo, b_o, Wy, b_y, out):
         by_row = keep.tile([P, STREAMS * OUT_FEAT], BF16)
         nc.vector.memset(by_row[:], 0.0)
 
+        nc.scalar.dma_start(out=bo_rows[0:STREAMS, :], in_=b_o)
         nc.scalar.dma_start(out=by_row[0:1, :], in_=b_y.rearrange("(o s) m -> o (s m)", o=1))
-        bo_bf16 = keep.tile([P, STREAMS * GATE_BLOCKS], BF16)
-        nc.scalar.dma_start(
-            out=bo_bf16[:].rearrange("p (s t) -> p s t", t=GATE_BLOCKS),
-            in_=b_o.rearrange("s (p t) -> p s t", t=GATE_BLOCKS),
-        )
         c_raw = keep.tile([P, 2 * HID], BF16)
         nc.sync.dma_start(out=c_raw[:], in_=c_view)
         wy_raw = keep.tile([P, 2 * STREAMS, HID], BF16)
-        nc.sync.dma_start(out=wy_raw[:], in_=wy_view)
+        for part in (slice(0, STREAMS), slice(STREAMS, 2 * STREAMS)):
+            nc.sync.dma_start(out=wy_raw[:, part, :], in_=wy_view[:, part, :])
         for i in range(RAW_BUFS):
             load(i)
 
-        bias_o = keep.tile([P, STREAMS * GATE_BLOCKS], F32)
-        nc.vector.tensor_copy(out=bias_o[:], in_=bo_bf16[:])
+        warm = keep.tile([P, 1], F32)
+        nc.scalar.activation(out=warm[:], in_=ones[:, 0:1], func=ACT.Sigmoid)
 
-        bias_y = keep.tile([P, STREAMS, OUT_FEAT], F32)
-        for half in range(STREAMS * OUT_FEAT // BANK):
-            spread = flip_psum.tile([P, BANK], F32, tag="flipped")
-            nc.tensor.matmul(
-                out=spread[:], lhsT=ones[:], rhs=by_row[:, half * BANK : (half + 1) * BANK],
-                start=True, stop=True,
-            )
-            nc.vector.tensor_copy(
-                out=bias_y[:].rearrange("p s m -> p (s m)")[:, half * BANK : (half + 1) * BANK],
-                in_=spread[:],
-            )
+        bo_words = bo_rows[:].bitcast(F32).rearrange("r (p u) -> r u p", u=2)
+        bo_flipped = flip_psum.tile([P, BANK], F32, tag="flipped")
+        for u in range(2):
+            nc.tensor.transpose(bo_flipped[:, u * P : (u + 1) * P], bo_words[:, u, :], ident[:])
+        bias_o = keep.tile([P, STREAMS * GATE_BLOCKS], F32)
+        nc.vector.tensor_copy(
+            out=bias_o[:].rearrange("p (s u e) -> p s u e", u=2, e=2),
+            in_=bo_flipped[:, 0 : 2 * P].bitcast(BF16).rearrange(
+                "p (u r e) -> p r u e", u=2, e=2
+            )[:, 0:STREAMS],
+        )
 
         c_words = c_raw[:].bitcast(F32).rearrange("r (b p u) -> r b u p", b=2, u=2)
         c_flipped = flip_psum.tile([P, BANK], F32, tag="flipped")
@@ -264,11 +263,27 @@ def tile_flatlstm_pb_k_kernel(tc, modulation, h0, c_new, Wo, b_o, Wy, b_y, out):
             in_=wy_grouped[:],
         )
 
+        bias_y = keep.tile([P, STREAMS, OUT_FEAT], F32)
+
+        def spread_bias_y():
+            for half in range(STREAMS * OUT_FEAT // BANK):
+                spread = flip_psum.tile([P, BANK], F32, tag="flipped")
+                nc.tensor.matmul(
+                    out=spread[:], lhsT=ones[:], rhs=by_row[:, half * BANK : (half + 1) * BANK],
+                    start=True, stop=True,
+                )
+                nc.vector.tensor_copy(
+                    out=bias_y[:].rearrange("p s m -> p (s m)")[:, half * BANK : (half + 1) * BANK],
+                    in_=spread[:],
+                )
+
         for i in range(N_CHUNKS + 3):
             if 0 <= i - 1 < N_CHUNKS:
                 quantise(i - 1)
             if i < N_CHUNKS:
                 flip(i)
+            if i == 1:
+                spread_bias_y()
             if i + RAW_BUFS < N_CHUNKS:
                 load(i + RAW_BUFS)
             if 0 <= i - 2 < N_CHUNKS:

@@ -27,15 +27,28 @@ DEPTH = X_FEAT + HID
 FLOPS = 2 * ROWS * STREAMS * (DEPTH * HID + HID * OUT_FEAT)
 
 CHUNK = DEPTH // 2
-CHUNK_PASSES = CHUNK // K_PASS
-CHUNK_BANKS = CHUNK // 2 // BANK
-CHUNK_WORDS = CHUNK // PACK
 GATE_BLOCKS = HID // P
 PAIR_UNITS = 1 + 2 * GATE_BLOCKS
-N_CHUNKS = 2 * PAIR_UNITS * 2
+N_UNITS = 2 * PAIR_UNITS
+WHOLE = (CHUNK, CHUNK)
+TAPERED = (2048, 2048, 2048, 1024, 1024)
+
+
+def cut_chunks():
+    chunks = []
+    for unit in range(N_UNITS):
+        first = 0
+        for width in WHOLE if unit < N_UNITS - 1 else TAPERED:
+            chunks.append((unit, first, width))
+            first += width
+    return chunks
+
+
+CHUNKS = cut_chunks()
+N_CHUNKS = len(CHUNKS)
 
 RAW_BUFS = 12
-VECTOR_BANK = 2
+MULTIPLY_LAG = 2 * CHUNK
 
 
 def tile_flatlstm_pb_k_kernel(tc, modulation, h0, c_new, Wo, b_o, Wy, b_y, out):
@@ -45,34 +58,34 @@ def tile_flatlstm_pb_k_kernel(tc, modulation, h0, c_new, Wo, b_o, Wy, b_y, out):
     h_view = h0.rearrange("n (a b l) -> (n a) b l", a=2, b=2)
     c_view = c_new.rearrange("n (a c) -> (n a) c", a=2)
     wo_view = Wo.rearrange("s (j t) k -> s t j k", t=GATE_BLOCKS)
-    wy_view = Wy.rearrange("s (h m) k -> m (s h) k", m=P)
+    wy_view = Wy.rearrange("s (m h) k -> m s (h k)", m=P)
 
     with ExitStack() as ctx:
         keep = ctx.enter_context(tc.tile_pool(name="keep", bufs=1))
         raw_pool = ctx.enter_context(tc.tile_pool(name="raw", bufs=RAW_BUFS))
         grouped_pool = ctx.enter_context(tc.tile_pool(name="grouped", bufs=3))
         xh_pool = ctx.enter_context(tc.tile_pool(name="xh", bufs=2))
-        wo_pool = ctx.enter_context(tc.tile_pool(name="wo", bufs=3))
+        wo_pool = ctx.enter_context(tc.tile_pool(name="wo", bufs=6))
         gate_pool = ctx.enter_context(tc.tile_pool(name="gate", bufs=2))
         flip_psum = ctx.enter_context(tc.psum_pool(name="flip", bufs=6))
         sum_psum = ctx.enter_context(tc.psum_pool(name="sums", bufs=2))
         ctx.enter_context(tc.manual_schedule())
 
-        def flip_bank(blocks, dest_words, bank):
+        def flip_bank(blocks, dest_words, on_vector):
             flipped = flip_psum.tile([P, BANK], F32)
             for j, block in enumerate(blocks):
                 nc.tensor.transpose(flipped[:, j * P : (j + 1) * P], block, ident[:])
             src = flipped[:].rearrange("p (g u c) -> p g c u", g=2, u=2)
             dst = dest_words.rearrange("p (g c u) -> p g c u", g=2, u=2)
-            if bank % CHUNK_BANKS == VECTOR_BANK:
+            if on_vector:
                 nc.vector.tensor_copy(out=dst, in_=src)
             else:
                 nc.scalar.copy(out=dst, in_=src)
 
         def place(i):
-            unit, half = divmod(i, 2)
+            unit, first, width = CHUNKS[i]
             b, r = divmod(unit, PAIR_UNITS)
-            return b, r, half
+            return b, r, first, width
 
         def stream_block(b, r):
             a, t = divmod(r - 1, GATE_BLOCKS)
@@ -81,12 +94,12 @@ def tile_flatlstm_pb_k_kernel(tc, modulation, h0, c_new, Wo, b_o, Wy, b_y, out):
         raws, groupeds, xh_codes, wo_codes, sums, gates = {}, {}, {}, {}, {}, {}
 
         def load(i):
-            b, r, half = place(i)
+            b, r, first, width = place(i)
             raw = raw_pool.tile([P, CHUNK], BF16)
             if r > 0:
                 a, s, t = stream_block(b, r)
-                nc.sync.dma_start(out=raw[:], in_=wo_view[s, t, :, half * CHUNK : (half + 1) * CHUNK])
-            elif half == 0:
+                nc.sync.dma_start(out=raw[:, 0:width], in_=wo_view[s, t, :, first : first + width])
+            elif first == 0:
                 nc.sync.dma_start(out=raw[:], in_=x_view[:, b, 0:CHUNK])
             else:
                 nc.sync.dma_start(out=raw[:, 0 : X_FEAT - CHUNK], in_=x_view[:, b, CHUNK:X_FEAT])
@@ -94,56 +107,61 @@ def tile_flatlstm_pb_k_kernel(tc, modulation, h0, c_new, Wo, b_o, Wy, b_y, out):
             raws[i] = raw
 
         def flip(i):
+            b, r, first, width = place(i)
             raw_words = raws[i][:].bitcast(F32)
             grouped = grouped_pool.tile([P, CHUNK], BF16, align_bytes=64)
             grouped_words = grouped[:].bitcast(F32)
-            for bank in range(CHUNK_BANKS):
-                first = bank * BANK
-                blocks = [raw_words[:, first + j * P : first + (j + 1) * P] for j in range(4)]
-                flip_bank(blocks, grouped_words[:, first : first + BANK], bank)
+            banks = width // 2 // BANK
+            for bank in range(banks):
+                word = bank * BANK
+                blocks = [raw_words[:, word + j * P : word + (j + 1) * P] for j in range(4)]
+                flip_bank(blocks, grouped_words[:, word : word + BANK], banks > 1 and bank == banks // 2)
             groupeds[i] = grouped
 
         def quantise(i):
-            b, r, half = place(i)
+            b, r, first, width = place(i)
+            words = width // PACK
             if r == 0:
-                if half == 0:
-                    xq = xh_pool.tile([P, 2 * CHUNK_WORDS], U32, align_bytes=64)
-                    xs = xh_pool.tile([P, 2 * CHUNK_WORDS], U8, align_bytes=64)
+                if first == 0:
+                    xq = xh_pool.tile([P, DEPTH // PACK], U32, align_bytes=64)
+                    xs = xh_pool.tile([P, DEPTH // PACK], U8, align_bytes=64)
                     xh_codes[b] = (xq, xs)
                 xq, xs = xh_codes[b]
-                cols = slice(half * CHUNK_WORDS, (half + 1) * CHUNK_WORDS)
+                cols = slice(first // PACK, first // PACK + words)
                 codes, scales = xq[:, cols], xs[:, cols]
             else:
-                wq = wo_pool.tile([P, CHUNK_WORDS], U32, align_bytes=64)
-                ws = wo_pool.tile([P, CHUNK_WORDS], U8, align_bytes=64)
+                wq = wo_pool.tile([P, CHUNK // PACK], U32, align_bytes=64)
+                ws = wo_pool.tile([P, CHUNK // PACK], U8, align_bytes=64)
                 wo_codes[i] = (wq, ws)
-                codes, scales = wq[:], ws[:]
-            nc.vector.quantize_mx(out=codes.bitcast(FP8X4), scales=scales, in_=groupeds[i][:])
+                codes, scales = wq[:, 0:words], ws[:, 0:words]
+            nc.vector.quantize_mx(
+                out=codes.bitcast(FP8X4), scales=scales, in_=groupeds[i][:, 0:width]
+            )
 
         def multiply(i):
-            b, r, half = place(i)
+            b, r, first, width = place(i)
             if r == 0:
                 return
             a, s, t = stream_block(b, r)
             wq, ws = wo_codes[i]
             xq, xs = xh_codes[b]
-            if half == 0:
+            if first == 0:
                 acc = sum_psum.tile([P, P], F32, tag="sum")
                 sums[s] = acc
             acc = sums[s]
-            for g in range(CHUNK_PASSES):
+            for g in range(width // K_PASS):
                 w_cols = slice(g * P, (g + 1) * P)
-                x_cols = slice((half * CHUNK_PASSES + g) * P, (half * CHUNK_PASSES + g + 1) * P)
+                x_cols = slice((first // K_PASS + g) * P, (first // K_PASS + g + 1) * P)
                 nc.tensor.matmul_mx(
                     out=acc[:],
                     lhsT=wq[:, w_cols].bitcast(FP8X4),
                     lhsT_scale=ws[:, w_cols],
                     rhs=xq[:, x_cols].bitcast(FP8X4),
                     rhs_scale=xs[:, x_cols],
-                    start=(half == 0 and g == 0),
-                    stop=(half == 1 and g == CHUNK_PASSES - 1),
+                    start=(first == 0 and g == 0),
+                    stop=(first + (g + 1) * K_PASS == DEPTH),
                 )
-            if half == 0:
+            if first + width < DEPTH:
                 return
             if t == 0:
                 gate = gate_pool.tile([P, GATE_BLOCKS, ROWS], F32)
@@ -169,8 +187,8 @@ def tile_flatlstm_pb_k_kernel(tc, modulation, h0, c_new, Wo, b_o, Wy, b_y, out):
             )
 
         def project(i):
-            b, r, half = place(i)
-            if r == 0 or half == 0:
+            b, r, first, width = place(i)
+            if r == 0 or first + width < DEPTH:
                 return
             a, s, t = stream_block(b, r)
             if t < GATE_BLOCKS - 1:
@@ -187,7 +205,10 @@ def tile_flatlstm_pb_k_kernel(tc, modulation, h0, c_new, Wo, b_o, Wy, b_y, out):
             )
             y = gate_pool.tile([ROWS, OUT_FEAT], F32)
             nc.vector.tensor_tensor(
-                out=y[:], in0=y_sum[0:ROWS, :], in1=bias_y[0:ROWS, s, :], op=ALU.add
+                out=y[:].rearrange("n (m h) -> n m h", h=2),
+                in0=y_sum[0:ROWS, :].rearrange("n (h m) -> n m h", h=2),
+                in1=bias_y[0:ROWS, s, :].rearrange("n (m h) -> n m h", h=2),
+                op=ALU.add,
             )
             nc.sync.dma_start(out=out[:, s * OUT_FEAT : (s + 1) * OUT_FEAT], in_=y[:])
 
@@ -208,8 +229,8 @@ def tile_flatlstm_pb_k_kernel(tc, modulation, h0, c_new, Wo, b_o, Wy, b_y, out):
         nc.scalar.dma_start(out=by_row[0:1, :], in_=b_y.rearrange("(o s) m -> o (s m)", o=1))
         c_raw = keep.tile([P, 2 * HID], BF16)
         nc.sync.dma_start(out=c_raw[:], in_=c_view)
-        wy_raw = keep.tile([P, 2 * STREAMS, HID], BF16)
-        for part in (slice(0, STREAMS), slice(STREAMS, 2 * STREAMS)):
+        wy_raw = keep.tile([P, STREAMS, 2 * HID], BF16)
+        for part in (slice(0, 2), slice(2, STREAMS)):
             nc.sync.dma_start(out=wy_raw[:, part, :], in_=wy_view[:, part, :])
         for i in range(RAW_BUFS):
             load(i)
@@ -254,7 +275,7 @@ def tile_flatlstm_pb_k_kernel(tc, modulation, h0, c_new, Wo, b_o, Wy, b_y, out):
         wy_grouped_words = wy_grouped[:].bitcast(F32)
         for s in range(STREAMS):
             blocks = [wy_words[:, 2 * s + h, u, :] for h in range(2) for u in range(2)]
-            flip_bank(blocks, wy_grouped_words[:, s * BANK : (s + 1) * BANK], s)
+            flip_bank(blocks, wy_grouped_words[:, s * BANK : (s + 1) * BANK], s == 2)
         wyq = keep.tile([P, STREAMS, OUT_FEAT], U32, align_bytes=64)
         wys = keep.tile([P, STREAMS, OUT_FEAT], U8, align_bytes=64)
         nc.vector.quantize_mx(
@@ -277,16 +298,26 @@ def tile_flatlstm_pb_k_kernel(tc, modulation, h0, c_new, Wo, b_o, Wy, b_y, out):
                     in_=spread[:],
                 )
 
-        for i in range(N_CHUNKS + 3):
-            if 0 <= i - 1 < N_CHUNKS:
+        multiplied = 0
+        projected = 0
+        for i in range(N_CHUNKS):
+            if i > 0:
                 quantise(i - 1)
-            if i < N_CHUNKS:
-                flip(i)
+            flip(i)
             if i == 1:
                 spread_bias_y()
             if i + RAW_BUFS < N_CHUNKS:
                 load(i + RAW_BUFS)
-            if 0 <= i - 2 < N_CHUNKS:
-                multiply(i - 2)
-            if 0 <= i - 3 < N_CHUNKS:
-                project(i - 3)
+            ready = multiplied
+            while sum(width for unit, first, width in CHUNKS[ready + 1 : i + 1]) >= MULTIPLY_LAG:
+                multiply(ready)
+                ready += 1
+            while projected < multiplied:
+                project(projected)
+                projected += 1
+            multiplied = ready
+        quantise(N_CHUNKS - 1)
+        for i in range(multiplied, N_CHUNKS):
+            multiply(i)
+        for i in range(projected, N_CHUNKS):
+            project(i)

@@ -57,7 +57,7 @@ def tile_flatlstm_pb_k_kernel(tc, modulation, h0, c_new, Wo, b_o, Wy, b_y, out):
     x_view = modulation.rearrange("n (a b i) -> (n a) b i", a=2, b=2)
     h_view = h0.rearrange("n (a b l) -> (n a) b l", a=2, b=2)
     c_view = c_new.rearrange("n (a c) -> (n a) c", a=2)
-    wo_view = Wo.rearrange("s (j t) k -> s t j k", t=GATE_BLOCKS)
+    wo_view = Wo.rearrange("s (u j e) k -> s u e j k", u=2, e=2)
     wy_view = Wy.rearrange("s (m h) k -> m s (h k)", m=P)
 
     with ExitStack() as ctx:
@@ -98,7 +98,7 @@ def tile_flatlstm_pb_k_kernel(tc, modulation, h0, c_new, Wo, b_o, Wy, b_y, out):
             raw = raw_pool.tile([P, CHUNK], BF16)
             if r > 0:
                 a, s, t = stream_block(b, r)
-                nc.sync.dma_start(out=raw[:, 0:width], in_=wo_view[s, t, :, first : first + width])
+                nc.sync.dma_start(out=raw[:, 0:width], in_=wo_view[s, t // 2, t % 2, :, first : first + width])
             elif first == 0:
                 nc.sync.dma_start(out=raw[:], in_=x_view[:, b, 0:CHUNK])
             else:
@@ -238,7 +238,7 @@ def tile_flatlstm_pb_k_kernel(tc, modulation, h0, c_new, Wo, b_o, Wy, b_y, out):
         warm = keep.tile([P, 1], F32)
         nc.scalar.activation(out=warm[:], in_=ones[:, 0:1], func=ACT.Sigmoid)
 
-        bo_words = bo_rows[:].bitcast(F32).rearrange("r (p u) -> r u p", u=2)
+        bo_words = bo_rows[:].bitcast(F32).rearrange("r (u p) -> r u p", u=2)
         bo_flipped = flip_psum.tile([P, BANK], F32, tag="flipped")
         for u in range(2):
             nc.tensor.transpose(bo_flipped[:, u * P : (u + 1) * P], bo_words[:, u, :], ident[:])
@@ -250,7 +250,7 @@ def tile_flatlstm_pb_k_kernel(tc, modulation, h0, c_new, Wo, b_o, Wy, b_y, out):
             )[:, 0:STREAMS],
         )
 
-        c_words = c_raw[:].bitcast(F32).rearrange("r (b p u) -> r b u p", b=2, u=2)
+        c_words = c_raw[:].bitcast(F32).rearrange("r (b u p) -> r b u p", b=2, u=2)
         c_flipped = flip_psum.tile([P, BANK], F32, tag="flipped")
         for b in range(2):
             for u in range(2):
@@ -269,7 +269,7 @@ def tile_flatlstm_pb_k_kernel(tc, modulation, h0, c_new, Wo, b_o, Wy, b_y, out):
             )
 
         wy_words = wy_raw[:].rearrange("m r k -> m (r k)").bitcast(F32).rearrange(
-            "m (r p u) -> m r u p", r=2 * STREAMS, u=2
+            "m (r u p) -> m r u p", r=2 * STREAMS, u=2
         )
         wy_grouped = grouped_pool.tile([P, STREAMS * OUT_FEAT * PACK], BF16, align_bytes=64, tag="grouped")
         wy_grouped_words = wy_grouped[:].bitcast(F32)

@@ -19,6 +19,7 @@ BANK = 512
 
 ROWS = 64
 STREAMS = 4
+LAST_STREAM = STREAMS - 1
 X_FEAT = 7680
 HID = 512
 OUT_FEAT = 256
@@ -44,10 +45,17 @@ def cut_chunks():
     return chunks
 
 
+def load_widths(unit):
+    if unit == N_UNITS - 1:
+        return TAPERED
+    return (DEPTH,) if 0 < unit <= LAST_WHOLE_LOAD else WHOLE
+
+
 CHUNKS = cut_chunks()
 N_CHUNKS = len(CHUNKS)
 
-RAW_BUFS = 12
+RAW_BUFS = 7
+LAST_WHOLE_LOAD = PAIR_UNITS + 1
 MULTIPLY_LAG = 2 * CHUNK
 
 
@@ -93,22 +101,26 @@ def tile_flatlstm_pb_k_kernel(tc, modulation, h0, c_new, Wo, b_o, Wy, b_y, out):
 
         raws, groupeds, xh_codes, wo_codes, sums, gates = {}, {}, {}, {}, {}, {}
 
-        def load(i):
-            b, r, first, width = place(i)
-            raw = raw_pool.tile([P, CHUNK], BF16)
+        def load(unit):
+            b, r = divmod(unit, PAIR_UNITS)
+            raw = raw_pool.tile([P, DEPTH], BF16)
             if r > 0:
                 a, s, t = stream_block(b, r)
-                nc.sync.dma_start(out=raw[:, 0:width], in_=wo_view[s, t // 2, t % 2, :, first : first + width])
-            elif first == 0:
-                nc.sync.dma_start(out=raw[:], in_=x_view[:, b, 0:CHUNK])
+                source, end = wo_view[s, t // 2, t % 2], DEPTH
             else:
-                nc.sync.dma_start(out=raw[:, 0 : X_FEAT - CHUNK], in_=x_view[:, b, CHUNK:X_FEAT])
-                nc.sync.dma_start(out=raw[:, X_FEAT - CHUNK : CHUNK], in_=h_view[:, b, :])
-            raws[i] = raw
+                source, end = x_view[:, b, :], X_FEAT
+            first = 0
+            for width in load_widths(unit):
+                last = min(first + width, end)
+                nc.sync.dma_start(out=raw[:, first:last], in_=source[:, first:last])
+                first = last
+            if r == 0:
+                nc.sync.dma_start(out=raw[:, X_FEAT:DEPTH], in_=h_view[:, b, :])
+            raws[unit] = raw
 
         def flip(i):
-            b, r, first, width = place(i)
-            raw_words = raws[i][:].bitcast(F32)
+            unit, first, width = CHUNKS[i]
+            raw_words = raws[unit][:, first : first + width].bitcast(F32)
             grouped = grouped_pool.tile([P, CHUNK], BF16, align_bytes=64)
             grouped_words = grouped[:].bitcast(F32)
             banks = width // 2 // BANK
@@ -230,8 +242,12 @@ def tile_flatlstm_pb_k_kernel(tc, modulation, h0, c_new, Wo, b_o, Wy, b_y, out):
         c_raw = keep.tile([P, 2 * HID], BF16)
         nc.sync.dma_start(out=c_raw[:], in_=c_view)
         wy_raw = keep.tile([P, STREAMS, 2 * HID], BF16)
-        for part in (slice(0, 2), slice(2, STREAMS)):
+
+        def load_wy(part):
             nc.sync.dma_start(out=wy_raw[:, part, :], in_=wy_view[:, part, :])
+
+        load_wy(slice(0, 2))
+        load_wy(slice(2, LAST_STREAM))
         for i in range(RAW_BUFS):
             load(i)
 
@@ -271,19 +287,27 @@ def tile_flatlstm_pb_k_kernel(tc, modulation, h0, c_new, Wo, b_o, Wy, b_y, out):
         wy_words = wy_raw[:].rearrange("m r k -> m (r k)").bitcast(F32).rearrange(
             "m (r u p) -> m r u p", r=2 * STREAMS, u=2
         )
-        wy_grouped = grouped_pool.tile([P, STREAMS * OUT_FEAT * PACK], BF16, align_bytes=64, tag="grouped")
-        wy_grouped_words = wy_grouped[:].bitcast(F32)
-        for s in range(STREAMS):
-            blocks = [wy_words[:, 2 * s + h, u, :] for h in range(2) for u in range(2)]
-            flip_bank(blocks, wy_grouped_words[:, s * BANK : (s + 1) * BANK], s == 2)
         wyq = keep.tile([P, STREAMS, OUT_FEAT], U32, align_bytes=64)
         wys = keep.tile([P, STREAMS, OUT_FEAT], U8, align_bytes=64)
-        nc.vector.quantize_mx(
-            out=wyq[:].rearrange("p s m -> p (s m)").bitcast(FP8X4),
-            scales=wys[:].rearrange("p s m -> p (s m)"),
-            in_=wy_grouped[:],
-        )
 
+        def flip_wy(part):
+            wy_grouped = grouped_pool.tile([P, CHUNK], BF16, align_bytes=64, tag="grouped")
+            for j, s in enumerate(part):
+                blocks = [wy_words[:, 2 * s + h, u, :] for h in range(2) for u in range(2)]
+                words = wy_grouped[:].bitcast(F32)[:, j * BANK : (j + 1) * BANK]
+                flip_bank(blocks, words, len(part) > 1 and j == 1)
+            return wy_grouped
+
+        def quantise_wy(part, wy_grouped):
+            first, last = part[0], part[-1] + 1
+            nc.vector.quantize_mx(
+                out=wyq[:, first:last, :].rearrange("p s m -> p (s m)").bitcast(FP8X4),
+                scales=wys[:, first:last, :].rearrange("p s m -> p (s m)"),
+                in_=wy_grouped[:, 0 : len(part) * OUT_FEAT * PACK],
+            )
+
+        for part in ((0, 1), (2,)):
+            quantise_wy(part, flip_wy(part))
         bias_y = keep.tile([P, STREAMS, OUT_FEAT], F32)
 
         def spread_bias_y():
@@ -306,8 +330,11 @@ def tile_flatlstm_pb_k_kernel(tc, modulation, h0, c_new, Wo, b_o, Wy, b_y, out):
             flip(i)
             if i == 1:
                 spread_bias_y()
-            if i + RAW_BUFS < N_CHUNKS:
-                load(i + RAW_BUFS)
+            unit, first, width = CHUNKS[i]
+            if first + width == DEPTH and unit + RAW_BUFS < N_UNITS:
+                load(unit + RAW_BUFS)
+                if unit + RAW_BUFS == N_UNITS - 1:
+                    load_wy(slice(LAST_STREAM, STREAMS))
             ready = multiplied
             while sum(width for unit, first, width in CHUNKS[ready + 1 : i + 1]) >= MULTIPLY_LAG:
                 multiply(ready)
@@ -317,6 +344,7 @@ def tile_flatlstm_pb_k_kernel(tc, modulation, h0, c_new, Wo, b_o, Wy, b_y, out):
                 projected += 1
             multiplied = ready
         quantise(N_CHUNKS - 1)
+        quantise_wy((LAST_STREAM,), flip_wy((LAST_STREAM,)))
         for i in range(multiplied, N_CHUNKS):
             multiply(i)
         for i in range(projected, N_CHUNKS):

@@ -75,6 +75,7 @@ def tile_flatlstm_pb_k_kernel(tc, modulation, h0, c_new, Wo, b_o, Wy, b_y, out):
         xh_pool = ctx.enter_context(tc.tile_pool(name="xh", bufs=2))
         wo_pool = ctx.enter_context(tc.tile_pool(name="wo", bufs=6))
         gate_pool = ctx.enter_context(tc.tile_pool(name="gate", bufs=2))
+        y_pool = ctx.enter_context(tc.tile_pool(name="y", bufs=STREAMS))
         flip_psum = ctx.enter_context(tc.psum_pool(name="flip", bufs=6))
         sum_psum = ctx.enter_context(tc.psum_pool(name="sums", bufs=2))
         ctx.enter_context(tc.manual_schedule())
@@ -99,7 +100,7 @@ def tile_flatlstm_pb_k_kernel(tc, modulation, h0, c_new, Wo, b_o, Wy, b_y, out):
             a, t = divmod(r - 1, GATE_BLOCKS)
             return a, 2 * a + b, t
 
-        raws, groupeds, xh_codes, wo_codes, sums, gates = {}, {}, {}, {}, {}, {}
+        raws, groupeds, xh_codes, wo_codes, sums, gates, ys = {}, {}, {}, {}, {}, {}, {}
 
         def load(unit):
             b, r = divmod(unit, PAIR_UNITS)
@@ -127,7 +128,8 @@ def tile_flatlstm_pb_k_kernel(tc, modulation, h0, c_new, Wo, b_o, Wy, b_y, out):
             for bank in range(banks):
                 word = bank * BANK
                 blocks = [raw_words[:, word + j * P : word + (j + 1) * P] for j in range(4)]
-                flip_bank(blocks, grouped_words[:, word : word + BANK], banks > 1 and bank == banks // 2)
+                on_vector = banks > 1 and bank == banks // 2 and i % 4 != 3
+                flip_bank(blocks, grouped_words[:, word : word + BANK], on_vector)
             groupeds[i] = grouped
 
         def quantise(i):
@@ -215,14 +217,17 @@ def tile_flatlstm_pb_k_kernel(tc, modulation, h0, c_new, Wo, b_o, Wy, b_y, out):
                 start=True,
                 stop=True,
             )
-            y = gate_pool.tile([ROWS, OUT_FEAT], F32)
+            y = y_pool.tile([ROWS, OUT_FEAT], F32)
             nc.vector.tensor_tensor(
                 out=y[:].rearrange("n (m h) -> n m h", h=2),
                 in0=y_sum[0:ROWS, :].rearrange("n (h m) -> n m h", h=2),
                 in1=bias_y[0:ROWS, s, :].rearrange("n (m h) -> n m h", h=2),
                 op=ALU.add,
             )
-            nc.sync.dma_start(out=out[:, s * OUT_FEAT : (s + 1) * OUT_FEAT], in_=y[:])
+            ys[s] = y
+
+        def store(s):
+            nc.sync.dma_start(out=out[:, s * OUT_FEAT : (s + 1) * OUT_FEAT], in_=ys[s][:])
 
         ident = keep.tile([P, P], F32)
         make_identity(nc, ident[:])
@@ -317,7 +322,7 @@ def tile_flatlstm_pb_k_kernel(tc, modulation, h0, c_new, Wo, b_o, Wy, b_y, out):
                     out=spread[:], lhsT=ones[:], rhs=by_row[:, half * BANK : (half + 1) * BANK],
                     start=True, stop=True,
                 )
-                nc.vector.tensor_copy(
+                nc.scalar.copy(
                     out=bias_y[:].rearrange("p s m -> p (s m)")[:, half * BANK : (half + 1) * BANK],
                     in_=spread[:],
                 )
@@ -336,9 +341,10 @@ def tile_flatlstm_pb_k_kernel(tc, modulation, h0, c_new, Wo, b_o, Wy, b_y, out):
                 if unit + RAW_BUFS == N_UNITS - 1:
                     load_wy(slice(LAST_STREAM, STREAMS))
             ready = multiplied
-            while sum(width for unit, first, width in CHUNKS[ready + 1 : i + 1]) >= MULTIPLY_LAG:
-                multiply(ready)
-                ready += 1
+            if first + width == DEPTH or unit == N_UNITS - 1:
+                while sum(w for n, f, w in CHUNKS[ready + 1 : i + 1]) >= MULTIPLY_LAG:
+                    multiply(ready)
+                    ready += 1
             while projected < multiplied:
                 project(projected)
                 projected += 1
@@ -347,5 +353,8 @@ def tile_flatlstm_pb_k_kernel(tc, modulation, h0, c_new, Wo, b_o, Wy, b_y, out):
         quantise_wy((LAST_STREAM,), flip_wy((LAST_STREAM,)))
         for i in range(multiplied, N_CHUNKS):
             multiply(i)
+        for s in sorted(ys):
+            store(s)
         for i in range(projected, N_CHUNKS):
             project(i)
+        store(LAST_STREAM)

@@ -128,7 +128,7 @@ def tile_flatlstm_pb_k_kernel(tc, modulation, h0, c_new, Wo, b_o, Wy, b_y, out):
             for bank in range(banks):
                 word = bank * BANK
                 blocks = [raw_words[:, word + j * P : word + (j + 1) * P] for j in range(4)]
-                on_vector = banks > 1 and bank == banks // 2 and i % 4 != 3
+                on_vector = bank == banks // 2 and i % 4 != 3 and unit < N_UNITS - 1
                 flip_bank(blocks, grouped_words[:, word : word + BANK], on_vector)
             groupeds[i] = grouped
 
@@ -259,18 +259,6 @@ def tile_flatlstm_pb_k_kernel(tc, modulation, h0, c_new, Wo, b_o, Wy, b_y, out):
         warm = keep.tile([P, 1], F32)
         nc.scalar.activation(out=warm[:], in_=ones[:, 0:1], func=ACT.Sigmoid)
 
-        bo_words = bo_rows[:].bitcast(F32).rearrange("r (u p) -> r u p", u=2)
-        bo_flipped = flip_psum.tile([P, BANK], F32, tag="flipped")
-        for u in range(2):
-            nc.tensor.transpose(bo_flipped[:, u * P : (u + 1) * P], bo_words[:, u, :], ident[:])
-        bias_o = keep.tile([P, STREAMS * GATE_BLOCKS], F32)
-        nc.vector.tensor_copy(
-            out=bias_o[:].rearrange("p (s u e) -> p s u e", u=2, e=2),
-            in_=bo_flipped[:, 0 : 2 * P].bitcast(BF16).rearrange(
-                "p (u r e) -> p r u e", u=2, e=2
-            )[:, 0:STREAMS],
-        )
-
         c_words = c_raw[:].bitcast(F32).rearrange("r (b u p) -> r b u p", b=2, u=2)
         c_flipped = flip_psum.tile([P, BANK], F32, tag="flipped")
         for b in range(2):
@@ -313,6 +301,20 @@ def tile_flatlstm_pb_k_kernel(tc, modulation, h0, c_new, Wo, b_o, Wy, b_y, out):
 
         for part in ((0, 1), (2,)):
             quantise_wy(part, flip_wy(part))
+
+        bo_words = bo_rows[:].bitcast(F32).rearrange("r (u p) -> r u p", u=2)
+        bo_flipped = flip_psum.tile([P, BANK], F32, tag="flipped")
+        for u in range(2):
+            nc.tensor.transpose(bo_flipped[:, u * P : (u + 1) * P], bo_words[:, u, :], ident[:])
+        bias_o = keep.tile([P, STREAMS * GATE_BLOCKS], F32)
+        nc.vector.tensor_copy(
+            out=bias_o[:].rearrange("p (s u e) -> p s u e", u=2, e=2),
+            in_=bo_flipped[:, 0 : 2 * P].bitcast(BF16).rearrange(
+                "p (u r e) -> p r u e", u=2, e=2
+            )[:, 0:STREAMS],
+        )
+
+
         bias_y = keep.tile([P, STREAMS, OUT_FEAT], F32)
 
         def spread_bias_y():

@@ -32,7 +32,7 @@ GATE_BLOCKS = HID // P
 PAIR_UNITS = 1 + 2 * GATE_BLOCKS
 N_UNITS = 2 * PAIR_UNITS
 WHOLE = (CHUNK, CHUNK)
-TAPERED = (2048, 2048, 2048, 1024, 1024)
+TAPERED = (4096, 2048, 1024, 1024)
 
 
 def cut_chunks():
@@ -48,7 +48,7 @@ def cut_chunks():
 def load_widths(unit):
     if unit == N_UNITS - 1:
         return TAPERED
-    return (DEPTH,) if 0 < unit <= LAST_WHOLE_LOAD else WHOLE
+    return (DEPTH,) if 1 < unit <= LAST_WHOLE_LOAD else WHOLE
 
 
 CHUNKS = cut_chunks()
@@ -63,7 +63,7 @@ def tile_flatlstm_pb_k_kernel(tc, modulation, h0, c_new, Wo, b_o, Wy, b_y, out):
     nc = tc.nc
 
     x_view = modulation.rearrange("n (a b i) -> (n a) b i", a=2, b=2)
-    h_view = h0.rearrange("n (a b l) -> (n a) b l", a=2, b=2)
+    h_view = h0.rearrange("n (a h) -> (n a) h", a=2)
     c_view = c_new.rearrange("n (a c) -> (n a) c", a=2)
     wo_view = Wo.rearrange("s (u j e) k -> s u e j k", u=2, e=2)
     wy_view = Wy.rearrange("s (m h) k -> m s (h k)", m=P)
@@ -115,21 +115,26 @@ def tile_flatlstm_pb_k_kernel(tc, modulation, h0, c_new, Wo, b_o, Wy, b_y, out):
                 last = min(first + width, end)
                 nc.sync.dma_start(out=raw[:, first:last], in_=source[:, first:last])
                 first = last
-            if r == 0:
-                nc.sync.dma_start(out=raw[:, X_FEAT:DEPTH], in_=h_view[:, b, :])
             raws[unit] = raw
 
         def flip(i):
             unit, first, width = CHUNKS[i]
-            raw_words = raws[unit][:, first : first + width].bitcast(F32)
+            b, r = divmod(unit, PAIR_UNITS)
+            raw_words = raws[unit][:].bitcast(F32)
+            h_words = h_raw[:, b, :].bitcast(F32)
             grouped = grouped_pool.tile([P, CHUNK], BF16, align_bytes=64)
             grouped_words = grouped[:].bitcast(F32)
             banks = width // 2 // BANK
             for bank in range(banks):
-                word = bank * BANK
-                blocks = [raw_words[:, word + j * P : word + (j + 1) * P] for j in range(4)]
+                blocks = []
+                for word in range((first + bank * 2 * BANK) // 2, (first + (bank + 1) * 2 * BANK) // 2, P):
+                    if r == 0 and word >= X_FEAT // 2:
+                        blocks.append(h_words[:, word - X_FEAT // 2 : word - X_FEAT // 2 + P])
+                    else:
+                        blocks.append(raw_words[:, word : word + P])
+                words = slice(bank * BANK, (bank + 1) * BANK)
                 on_vector = bank == banks // 2 and i % 4 != 3 and unit < N_UNITS - 1
-                flip_bank(blocks, grouped_words[:, word : word + BANK], on_vector)
+                flip_bank(blocks, grouped_words[:, words], on_vector)
             groupeds[i] = grouped
 
         def quantise(i):
@@ -253,7 +258,10 @@ def tile_flatlstm_pb_k_kernel(tc, modulation, h0, c_new, Wo, b_o, Wy, b_y, out):
 
         load_wy(slice(0, 2))
         load_wy(slice(2, LAST_STREAM))
-        for i in range(RAW_BUFS):
+        h_raw = keep.tile([P, 2, HID], BF16)
+        load(0)
+        nc.sync.dma_start(out=h_raw[:].rearrange("p b l -> p (b l)"), in_=h_view)
+        for i in range(1, RAW_BUFS):
             load(i)
 
         warm = keep.tile([P, 1], F32)
@@ -343,10 +351,9 @@ def tile_flatlstm_pb_k_kernel(tc, modulation, h0, c_new, Wo, b_o, Wy, b_y, out):
                 if unit + RAW_BUFS == N_UNITS - 1:
                     load_wy(slice(LAST_STREAM, STREAMS))
             ready = multiplied
-            if first + width == DEPTH or unit == N_UNITS - 1:
-                while sum(w for n, f, w in CHUNKS[ready + 1 : i + 1]) >= MULTIPLY_LAG:
-                    multiply(ready)
-                    ready += 1
+            while sum(w for n, f, w in CHUNKS[ready + 1 : i + 1]) >= MULTIPLY_LAG:
+                multiply(ready)
+                ready += 1
             while projected < multiplied:
                 project(projected)
                 projected += 1

@@ -133,7 +133,7 @@ def tile_flatlstm_pb_k_kernel(tc, modulation, h0, c_new, Wo, b_o, Wy, b_y, out):
                     else:
                         blocks.append(raw_words[:, word : word + P])
                 words = slice(bank * BANK, (bank + 1) * BANK)
-                on_vector = bank == banks // 2 and i % 4 != 3 and unit < N_UNITS - 1
+                on_vector = bank == banks // 2 and i % 4 != 0 and unit < N_UNITS - 1
                 flip_bank(blocks, grouped_words[:, words], on_vector)
             groupeds[i] = grouped
 

from contextlib import ExitStack

import concourse.mybir as mybir
from concourse.masks import make_identity

F32 = mybir.dt.float32
BF16 = mybir.dt.bfloat16
U32 = mybir.dt.uint32
U8 = mybir.dt.uint8
I32 = mybir.dt.int32
FP8X4 = mybir.dt.float8_e4m3fn_x4
ACT = mybir.ActivationFunctionType
ALU = mybir.AluOpType

P = 128
PACK = 4
K_PASS = P * PACK
BANK = 512

ROWS = 64
STREAMS = 4
LAST_STREAM = STREAMS - 1
X_FEAT = 7680
HID = 512
OUT_FEAT = 256
DEPTH = X_FEAT + HID

FLOPS = 2 * ROWS * STREAMS * (DEPTH * HID + HID * OUT_FEAT)

CHUNK = DEPTH // 2
GATE_BLOCKS = HID // P
PAIR_UNITS = 1 + 2 * GATE_BLOCKS
N_UNITS = 2 * PAIR_UNITS
WHOLE = (CHUNK, CHUNK)
TAPERED = (4096, 2048, 1024, 1024)


def cut_chunks():
    chunks = []
    for unit in range(N_UNITS):
        first = 0
        for width in WHOLE if unit < N_UNITS - 1 else TAPERED:
            chunks.append((unit, first, width))
            first += width
    return chunks


def load_widths(unit):
    if unit == N_UNITS - 1:
        return TAPERED
    return (DEPTH,) if 1 < unit <= LAST_WHOLE_LOAD else WHOLE


CHUNKS = cut_chunks()
N_CHUNKS = len(CHUNKS)

RAW_BUFS = 7
LAST_WHOLE_LOAD = PAIR_UNITS + 1
MULTIPLY_LAG = 2 * CHUNK


def tile_flatlstm_pb_k_kernel(tc, modulation, h0, c_new, Wo, b_o, Wy, b_y, out):
    nc = tc.nc

    x_view = modulation.rearrange("n (a b i) -> (n a) b i", a=2, b=2)
    h_view = h0.rearrange("n (a h) -> (n a) h", a=2)
    c_view = c_new.rearrange("n (a c) -> (n a) c", a=2)
    wo_view = Wo.rearrange("s (u j e) k -> s u e j k", u=2, e=2)
    wy_view = Wy.rearrange("s (m h) k -> m s (h k)", m=P)

    with ExitStack() as ctx:
        keep = ctx.enter_context(tc.tile_pool(name="keep", bufs=1))
        raw_pool = ctx.enter_context(tc.tile_pool(name="raw", bufs=RAW_BUFS))
        grouped_pool = ctx.enter_context(tc.tile_pool(name="grouped", bufs=3))
        xh_pool = ctx.enter_context(tc.tile_pool(name="xh", bufs=2))
        wo_pool = ctx.enter_context(tc.tile_pool(name="wo", bufs=6))
        gate_pool = ctx.enter_context(tc.tile_pool(name="gate", bufs=2))
        y_pool = ctx.enter_context(tc.tile_pool(name="y", bufs=STREAMS))
        flip_psum = ctx.enter_context(tc.psum_pool(name="flip", bufs=6))
        sum_psum = ctx.enter_context(tc.psum_pool(name="sums", bufs=2))
        ctx.enter_context(tc.manual_schedule())

        def flip_bank(blocks, dest_words, on_vector):
            flipped = flip_psum.tile([P, BANK], F32)
            for j, block in enumerate(blocks):
                nc.tensor.transpose(flipped[:, j * P : (j + 1) * P], block, ident[:])
            src = flipped[:].rearrange("p (g u c) -> p g c u", g=2, u=2)
            dst = dest_words.rearrange("p (g c u) -> p g c u", g=2, u=2)
            if on_vector:
                nc.vector.tensor_copy(out=dst, in_=src)
            else:
                nc.scalar.copy(out=dst, in_=src)

        def place(i):
            unit, first, width = CHUNKS[i]
            b, r = divmod(unit, PAIR_UNITS)
            return b, r, first, width

        def stream_block(b, r):
            a, t = divmod(r - 1, GATE_BLOCKS)
            return a, 2 * a + b, t

        raws, groupeds, xh_codes, wo_codes, sums, gates, ys = {}, {}, {}, {}, {}, {}, {}

        def load(unit):
            b, r = divmod(unit, PAIR_UNITS)
            raw = raw_pool.tile([P, DEPTH], BF16)
            if r > 0:
                a, s, t = stream_block(b, r)
                source, end = wo_view[s, t // 2, t % 2], DEPTH
            else:
                source, end = x_view[:, b, :], X_FEAT
            first = 0
            for width in load_widths(unit):
                last = min(first + width, end)
                nc.sync.dma_start(out=raw[:, first:last], in_=source[:, first:last])
                first = last
            raws[unit] = raw

        def flip(i):
            unit, first, width = CHUNKS[i]
            b, r = divmod(unit, PAIR_UNITS)
            raw_words = raws[unit][:].bitcast(F32)
            h_words = h_raw[:, b, :].bitcast(F32)
            grouped = grouped_pool.tile([P, CHUNK], BF16, align_bytes=64)
            grouped_words = grouped[:].bitcast(F32)
            banks = width // 2 // BANK
            for bank in range(banks):
                blocks = []
                for word in range((first + bank * 2 * BANK) // 2, (first + (bank + 1) * 2 * BANK) // 2, P):
                    if r == 0 and word >= X_FEAT // 2:
                        blocks.append(h_words[:, word - X_FEAT // 2 : word - X_FEAT // 2 + P])
                    else:
                        blocks.append(raw_words[:, word : word + P])
                words = slice(bank * BANK, (bank + 1) * BANK)
                on_vector = bank == banks // 2 and i % 4 != 0 and unit < N_UNITS - 1
                flip_bank(blocks, grouped_words[:, words], on_vector)
            groupeds[i] = grouped

        def quantise(i):
            b, r, first, width = place(i)
            words = width // PACK
            if r == 0:
                if first == 0:
                    xq = xh_pool.tile([P, DEPTH // PACK], U32, align_bytes=64)
                    xs = xh_pool.tile([P, DEPTH // PACK], U8, align_bytes=64)
                    xh_codes[b] = (xq, xs)
                xq, xs = xh_codes[b]
                cols = slice(first // PACK, first // PACK + words)
                codes, scales = xq[:, cols], xs[:, cols]
            else:
                wq = wo_pool.tile([P, CHUNK // PACK], U32, align_bytes=64)
                ws = wo_pool.tile([P, CHUNK // PACK], U8, align_bytes=64)
                wo_codes[i] = (wq, ws)
                codes, scales = wq[:, 0:words], ws[:, 0:words]
            nc.vector.quantize_mx(
                out=codes.bitcast(FP8X4), scales=scales, in_=groupeds[i][:, 0:width]
            )

        def multiply(i):
            b, r, first, width = place(i)
            if r == 0:
                return
            a, s, t = stream_block(b, r)
            wq, ws = wo_codes[i]
            xq, xs = xh_codes[b]
            if first == 0:
                acc = sum_psum.tile([P, P], F32, tag="sum")
                sums[s] = acc
            acc = sums[s]
            for g in range(width // K_PASS):
                w_cols = slice(g * P, (g + 1) * P)
                x_cols = slice((first // K_PASS + g) * P, (first // K_PASS + g + 1) * P)
                nc.tensor.matmul_mx(
                    out=acc[:],
                    lhsT=wq[:, w_cols].bitcast(FP8X4),
                    lhsT_scale=ws[:, w_cols],
                    rhs=xq[:, x_cols].bitcast(FP8X4),
                    rhs_scale=xs[:, x_cols],
                    start=(first == 0 and g == 0),
                    stop=(first + (g + 1) * K_PASS == DEPTH),
                )
            if first + width < DEPTH:
                return
            if t == 0:
                gate = gate_pool.tile([P, GATE_BLOCKS, ROWS], F32)
                gates[s] = gate
            gate = gates[s]
            nc.scalar.activation(
                out=gate[:, t, :],
                in_=acc[:].rearrange("p (n a) -> p a n", a=2)[:, a, :],
                func=ACT.Sigmoid,
                bias=bias_o[:, s * GATE_BLOCKS + t : s * GATE_BLOCKS + t + 1],
            )
            if t < GATE_BLOCKS - 1:
                return
            h_new = gate_pool.tile([P, ROWS * PACK], BF16, align_bytes=64)
            nc.vector.tensor_tensor(
                out=h_new[:].rearrange("p (n t) -> p n t", t=PACK),
                in0=gate[:].rearrange("p t n -> p n t"),
                in1=tanh_c[:, s, :].rearrange("p (n t) -> p n t", t=PACK),
                op=ALU.mult,
            )
            nc.vector.quantize_mx(
                out=hq[:, s, 0:ROWS].bitcast(FP8X4), scales=hs[:, s, 0:ROWS], in_=h_new[:]
            )

        def project(i):
            b, r, first, width = place(i)
            if r == 0 or first + width < DEPTH:
                return
            a, s, t = stream_block(b, r)
            if t < GATE_BLOCKS - 1:
                return
            y_sum = sum_psum.tile([P, OUT_FEAT], F32, tag="sum")
            nc.tensor.matmul_mx(
                out=y_sum[:],
                lhsT=hq[:, s, :].bitcast(FP8X4),
                lhsT_scale=hs[:, s, :],
                rhs=wyq[:, s, :].bitcast(FP8X4),
                rhs_scale=wys[:, s, :],
                start=True,
                stop=True,
            )
            y = y_pool.tile([ROWS, OUT_FEAT], F32)
            nc.vector.tensor_tensor(
                out=y[:].rearrange("n (m h) -> n m h", h=2),
                in0=y_sum[0:ROWS, :].rearrange("n (h m) -> n m h", h=2),
                in1=bias_y[0:ROWS, s, :].rearrange("n (m h) -> n m h", h=2),
                op=ALU.add,
            )
            ys[s] = y

        def store(s):
            nc.sync.dma_start(out=out[:, s * OUT_FEAT : (s + 1) * OUT_FEAT], in_=ys[s][:])

        ident = keep.tile([P, P], F32)
        make_identity(nc, ident[:])
        ones = keep.tile([P, P], BF16)
        nc.vector.memset(ones[:], 1.0)
        bo_rows = keep.tile([P, HID], BF16)
        nc.vector.memset(bo_rows[:], 0.0)
        hq = keep.tile([P, STREAMS, P], U32, align_bytes=64)
        hs = keep.tile([P, STREAMS, P], U8, align_bytes=64)
        nc.vector.memset(hq[:].bitcast(I32), 0)
        nc.vector.memset(hs[:].bitcast(I32), 0)
        by_row = keep.tile([P, STREAMS * OUT_FEAT], BF16)
        nc.vector.memset(by_row[:], 0.0)

        nc.scalar.dma_start(out=bo_rows[0:STREAMS, :], in_=b_o)
        nc.scalar.dma_start(out=by_row[0:1, :], in_=b_y.rearrange("(o s) m -> o (s m)", o=1))
        c_raw = keep.tile([P, 2 * HID], BF16)
        nc.sync.dma_start(out=c_raw[:], in_=c_view)
        wy_raw = keep.tile([P, STREAMS, 2 * HID], BF16)

        def load_wy(part):
            nc.sync.dma_start(out=wy_raw[:, part, :], in_=wy_view[:, part, :])

        load_wy(slice(0, 2))
        load_wy(slice(2, LAST_STREAM))
        h_raw = keep.tile([P, 2, HID], BF16)
        load(0)
        nc.sync.dma_start(out=h_raw[:].rearrange("p b l -> p (b l)"), in_=h_view)
        for i in range(1, RAW_BUFS):
            load(i)

        warm = keep.tile([P, 1], F32)
        nc.scalar.activation(out=warm[:], in_=ones[:, 0:1], func=ACT.Sigmoid)

        c_words = c_raw[:].bitcast(F32).rearrange("r (b u p) -> r b u p", b=2, u=2)
        c_flipped = flip_psum.tile([P, BANK], F32, tag="flipped")
        for b in range(2):
            for u in range(2):
                j = 2 * b + u
                nc.tensor.transpose(c_flipped[:, j * P : (j + 1) * P], c_words[:, b, u, :], ident[:])
        c_values = c_flipped[:].bitcast(BF16).rearrange(
            "p (b u n a e) -> p b a n u e", b=2, u=2, a=2, e=2
        )
        tanh_c = keep.tile([P, STREAMS, ROWS * PACK], F32)
        for s in range(STREAMS):
            a, b = divmod(s, 2)
            nc.scalar.activation(
                out=tanh_c[:, s, :].rearrange("p (n u e) -> p n u e", u=2, e=2),
                in_=c_values[:, b, a],
                func=ACT.Tanh,
            )

        wy_words = wy_raw[:].rearrange("m r k -> m (r k)").bitcast(F32).rearrange(
            "m (r u p) -> m r u p", r=2 * STREAMS, u=2
        )
        wyq = keep.tile([P, STREAMS, OUT_FEAT], U32, align_bytes=64)
        wys = keep.tile([P, STREAMS, OUT_FEAT], U8, align_bytes=64)

        def flip_wy(part):
            wy_grouped = grouped_pool.tile([P, CHUNK], BF16, align_bytes=64, tag="grouped")
            for j, s in enumerate(part):
                blocks = [wy_words[:, 2 * s + h, u, :] for h in range(2) for u in range(2)]
                words = wy_grouped[:].bitcast(F32)[:, j * BANK : (j + 1) * BANK]
                flip_bank(blocks, words, len(part) > 1 and j == 1)
            return wy_grouped

        def quantise_wy(part, wy_grouped):
            first, last = part[0], part[-1] + 1
            nc.vector.quantize_mx(
                out=wyq[:, first:last, :].rearrange("p s m -> p (s m)").bitcast(FP8X4),
                scales=wys[:, first:last, :].rearrange("p s m -> p (s m)"),
                in_=wy_grouped[:, 0 : len(part) * OUT_FEAT * PACK],
            )

        for part in ((0, 1), (2,)):
            quantise_wy(part, flip_wy(part))

        bo_words = bo_rows[:].bitcast(F32).rearrange("r (u p) -> r u p", u=2)
        bo_flipped = flip_psum.tile([P, BANK], F32, tag="flipped")
        for u in range(2):
            nc.tensor.transpose(bo_flipped[:, u * P : (u + 1) * P], bo_words[:, u, :], ident[:])
        bias_o = keep.tile([P, STREAMS * GATE_BLOCKS], F32)
        nc.vector.tensor_copy(
            out=bias_o[:].rearrange("p (s u e) -> p s u e", u=2, e=2),
            in_=bo_flipped[:, 0 : 2 * P].bitcast(BF16).rearrange(
                "p (u r e) -> p r u e", u=2, e=2
            )[:, 0:STREAMS],
        )


        bias_y = keep.tile([P, STREAMS, OUT_FEAT], F32)

        def spread_bias_y():
            for half in range(STREAMS * OUT_FEAT // BANK):
                spread = flip_psum.tile([P, BANK], F32, tag="flipped")
                nc.tensor.matmul(
                    out=spread[:], lhsT=ones[:], rhs=by_row[:, half * BANK : (half + 1) * BANK],
                    start=True, stop=True,
                )
                nc.scalar.copy(
                    out=bias_y[:].rearrange("p s m -> p (s m)")[:, half * BANK : (half + 1) * BANK],
                    in_=spread[:],
                )

        multiplied = 0
        projected = 0
        for i in range(N_CHUNKS):
            if i > 0:
                quantise(i - 1)
            flip(i)
            if i == 1:
                spread_bias_y()
            unit, first, width = CHUNKS[i]
            if first + width == DEPTH and unit + RAW_BUFS < N_UNITS:
                load(unit + RAW_BUFS)
                if unit + RAW_BUFS == N_UNITS - 1:
                    load_wy(slice(LAST_STREAM, STREAMS))
            ready = multiplied
            while sum(w for n, f, w in CHUNKS[ready + 1 : i + 1]) >= MULTIPLY_LAG:
                multiply(ready)
                ready += 1
            while projected < multiplied:
                project(projected)
                projected += 1
            multiplied = ready
        quantise(N_CHUNKS - 1)
        quantise_wy((LAST_STREAM,), flip_wy((LAST_STREAM,)))
        for i in range(multiplied, N_CHUNKS):
            multiply(i)
        for s in sorted(ys):
            store(s)
        for i in range(projected, N_CHUNKS):
            project(i)
        store(LAST_STREAM)
